import numpy as np
import ml_dtypes


def mxq(x, axis, fmt="e4m3"):
    dtype, down = {"e4m3": (ml_dtypes.float8_e4m3fn, 7), "e5m2": (ml_dtypes.float8_e5m2, 14)}[fmt]
    v = np.moveaxis(np.asarray(x, np.float32).astype(ml_dtypes.bfloat16).astype(np.float64), axis, -1)
    blocks = v.reshape(v.shape[:-1] + (-1, 32))
    amax = np.abs(blocks).max(-1, keepdims=True)
    byte = np.maximum(np.where(amax > 0, np.frexp(amax)[1] - 1 + 127, 0) - down, 1)
    scale = np.exp2(byte - 127.0)
    codes = (blocks / scale).astype(np.float32).astype(dtype).astype(np.float64)
    return np.moveaxis((codes * scale).reshape(v.shape), -1, axis)


WIDE = False


def mx_kscale(k):
    if not WIDE:
        return np.ones(k)
    levels = np.array([10, -10, 5, -5, 0])
    a = np.random.permutation(np.resize(levels, k // 512 * 4)).reshape(k // 512, 4)
    idx = np.arange(k)
    return np.exp2(a[idx // 512, idx % 128 // 32])


BF16 = ml_dtypes.bfloat16


def bf(x):
    return np.asarray(x, np.float32).astype(BF16)


def f64(x):
    return np.asarray(x).astype(np.float64)


B, D, U, G = 8192, 512, 1, 8


def band_mask(input_dim, units_per_sublayer, graph_distance):
    rows = np.arange(input_dim)[:, None]
    col_block = np.arange(input_dim * units_per_sublayer) // units_per_sublayer
    m = (rows >= col_block) & (rows <= col_block + graph_distance)
    return m.astype(np.float64)


def setup_inputs():
    s = mx_kscale(D)
    return {"x": bf(np.random.standard_normal((B, D)) * s),
            "W": bf(np.random.standard_normal((D, D * U)) * 0.8 / np.sqrt(G + 1) / s[:, None]),
            "b": bf(np.random.standard_normal(D * U) * 0.1),
            "units_per_sublayer": U, "graph_distance": G}


def reference(x, W, b, units_per_sublayer, graph_distance):
    Wf = f64(W)
    mask = band_mask(Wf.shape[0], units_per_sublayer, graph_distance)
    y = (mxq(f64(x), 1, "e4m3") @ mxq(Wf * mask, 0, "e4m3")) + f64(b)
    return np.tanh(y)

@@ -1,0 +1,223 @@
+from contextlib import ExitStack
+
+import concourse.mybir as mybir
+from concourse.masks import make_identity
+
+F32 = mybir.dt.float32
+BF16 = mybir.dt.bfloat16
+I32 = mybir.dt.int32
+U32 = mybir.dt.uint32
+U8 = mybir.dt.uint8
+FP8X4 = mybir.dt.float8_e4m3fn_x4
+ADD = mybir.AluOpType.add
+MULT = mybir.AluOpType.mult
+TANH = mybir.ActivationFunctionType.Tanh
+
+P = 128
+B = 8192
+D = 512
+FLOPS = 2 * B * D * D
+
+MANUAL = True
+GROUP_TILES = [2, 2, 4] + [8] * 7
+NT = B // P
+QT = 4
+NQ = NT // QT
+LC = 4
+V_COPY = ((6, 1), (9, 1), (12, 1), (15, 1))
+Y_BUFS = 8
+
+
+def tile_compositional_t_kernel(tc, x, W, b, units_per_sublayer, graph_distance, out):
+    nc = tc.nc
+    assert units_per_sublayer == 1 and graph_distance == 8
+    assert sum(GROUP_TILES) == NT
+
+    with ExitStack() as ctx:
+        const = ctx.enter_context(tc.tile_pool(name="const", bufs=1))
+        xpool = ctx.enter_context(tc.tile_pool(name="xpool", bufs=1))
+        gpool = ctx.enter_context(tc.tile_pool(name="gpool", bufs=4))
+        qpool = ctx.enter_context(tc.tile_pool(name="qpool", bufs=4))
+        ypool = ctx.enter_context(tc.tile_pool(name="ypool", bufs=Y_BUFS))
+        psum = ctx.enter_context(tc.psum_pool(name="psum", bufs=4))
+        if MANUAL:
+            ctx.enter_context(tc.manual_schedule())
+
+        bz = const.tile([P, D], BF16, name="bz")
+        nc.vector.memset(bz[:].bitcast(I32), 0)
+        nc.scalar.dma_start(out=bz[0:1, :], in_=b.rearrange("(o n) -> o n", o=1))
+
+        ident = const.tile([P, P], F32, name="ident")
+        make_identity(nc, ident[:])
+
+        warm_in = const.tile([P, 1], F32, name="warm_in")
+        warm_out = const.tile([P, 1], F32, name="warm_out")
+        nc.vector.memset(warm_in[:], 0.0)
+        nc.scalar.activation(out=warm_out[:], in_=warm_in[:], func=TANH)
+
+        wt = const.tile([P, 4 * D], BF16, name="wt")
+        nc.sync.dma_start(
+            out=wt[:].rearrange("p (u f) -> p u f", u=2),
+            in_=W.rearrange("(u q e) c -> q u (e c)", u=2, e=2),
+        )
+        xs = []
+        out_views = []
+        where = []
+        row0 = 0
+        for g, tiles in enumerate(GROUP_TILES):
+            rows = slice(row0, row0 + P * tiles)
+            xg = xpool.tile([P, tiles * D], BF16, name="x%d" % g)
+            nc.sync.dma_start(out=xg[:], in_=x[rows, :].rearrange("(p t) k -> p (t k)", t=tiles))
+            xs.append(xg)
+            out_views.append(out[rows, :].rearrange("(p t) n -> p (t n)", t=tiles))
+            where.extend([(g, t) for t in range(tiles)])
+            row0 += P * tiles
+
+        ones = const.tile([P, P], BF16, name="ones")
+        nc.vector.memset(ones[:], 1.0)
+        e1 = const.tile([P, 288], BF16, name="e1")
+        nc.vector.memset(e1[:].bitcast(I32), 0)
+        mask = const.tile([P, 4 * D], BF16, name="mask")
+        nc.vector.memset(mask[:].bitcast(I32), 0)
+        nc.vector.tensor_copy(
+            out=e1[:, 16:272].rearrange("p (c two) -> p c two", two=2)[:, :, 0], in_=ident[:]
+        )
+        b2 = const.tile([P, 288], BF16, name="b2")
+        b4 = const.tile([P, 288], BF16, name="b4")
+        b8 = const.tile([P, 288], BF16, name="b8")
+        b9 = const.tile([P, 288], BF16, name="b9")
+        nc.vector.tensor_tensor(out=b2[:, 0:278], in0=e1[:, 0:278], in1=e1[:, 1:279], op=ADD)
+        nc.vector.tensor_tensor(out=b4[:, 0:276], in0=b2[:, 0:276], in1=b2[:, 2:278], op=ADD)
+        nc.vector.tensor_tensor(out=b8[:, 0:272], in0=b4[:, 0:272], in1=b4[:, 4:276], op=ADD)
+        nc.vector.tensor_tensor(out=b9[:, 0:272], in0=b8[:, 0:272], in1=e1[:, 8:280], op=ADD)
+        nc.vector.tensor_copy(out=mask[:, 0:256], in_=b9[:, 16:272])
+        nc.vector.tensor_copy(out=mask[:, 512:768], in_=b9[:, 15:271])
+        nc.vector.tensor_copy(out=mask[:, 1272:1536], in_=b9[:, 8:272])
+        nc.vector.tensor_copy(out=mask[:, 1784:2048], in_=b9[:, 7:271])
+
+        bias_bc = const.tile([P, D], F32, name="bias_bc")
+
+        nc.vector.tensor_tensor(out=wt[:], in0=wt[:], in1=mask[:], op=MULT)
+        wg = const.tile([P, 4 * D], BF16, name="wg", align_bytes=64)
+        nc.vector.tensor_copy(
+            out=wg[:].rearrange("p (c i t) -> p c t i", i=4, t=4),
+            in_=wt[:].rearrange("p (t c i) -> p c t i", t=4, i=4),
+        )
+        w_codes = const.tile([P, D], U32, name="w_codes", align_bytes=64)
+        w_scales = const.tile([P, D], U8, name="w_scales", align_bytes=64)
+        nc.vector.quantize_mx(out=w_codes[:].bitcast(FP8X4), scales=w_scales[:], in_=wg[:])
+
+        banks = {}
+        grouped = {}
+        codes = {}
+        accs = {}
+        pieces = {}
+
+        def transposes(q):
+            for h in range(2):
+                tp = psum.tile([P, 2, 2, P], F32, tag="tp", name="tp")
+                banks[(q, h)] = tp
+                for j in range(2):
+                    g, t = where[QT * q + 2 * h + j]
+                    words = xs[g][:].bitcast(F32)
+                    for u in range(2):
+                        c0 = 256 * t + P * u
+                        nc.tensor.transpose(tp[:, j, u, :], words[:, c0 : c0 + P], ident[:])
+
+        def copies(q, on_vector):
+            if q not in grouped:
+                grouped[q] = gpool.tile([P, QT * D], BF16, tag="grp", name="grp", align_bytes=64)
+            g32 = grouped[q][:].bitcast(F32)
+            for h in range(2):
+                dst = g32[:, 512 * h : 512 * h + 512].rearrange("p (j r u) -> p j r u", j=2, u=2)
+                src = banks[(q, h)][:].rearrange("p j u r -> p j r u")
+                if on_vector and (q, h) in V_COPY:
+                    nc.vector.tensor_copy(out=dst, in_=src)
+                if not on_vector and (q, h) not in V_COPY:
+                    nc.scalar.copy(out=dst, in_=src)
+
+        def quantise(q):
+            cq = qpool.tile([P, QT * P], U32, tag="codes", name="codes", align_bytes=64)
+            sq = qpool.tile([P, QT * P], U8, tag="scales", name="scales", align_bytes=64)
+            codes[q] = (cq, sq)
+            nc.vector.quantize_mx(out=cq[:].bitcast(FP8X4), scales=sq[:], in_=grouped[q][:])
+
+        def passes(q):
+            cq, sq = codes[q]
+            for j in range(QT):
+                acc = psum.tile([P, D], F32, tag="mm", name="acc")
+                accs[(q, j)] = acc
+                cols = slice(P * j, P * j + P)
+                nc.tensor.matmul_mx(
+                    out=acc[:],
+                    lhsT=cq[:, cols].bitcast(FP8X4),
+                    lhsT_scale=sq[:, cols],
+                    rhs=w_codes[:].bitcast(FP8X4),
+                    rhs_scale=w_scales[:],
+                    start=True,
+                    stop=True,
+                )
+
+        def cut(q):
+            if q == NQ - 1:
+                sizes = [2, 1, 1]
+            elif q >= NQ - LC:
+                sizes = [2, 2]
+            elif where[QT * q][0] != where[QT * q + QT - 1][0]:
+                sizes = [2, 2]
+            else:
+                sizes = [4]
+            return sizes
+
+        def finish(piece):
+            y, g, t0, n = piece
+            nc.scalar.activation(out=y[:], in_=y[:], func=TANH)
+            nc.sync.dma_start(out=out_views[g][:, D * t0 : D * (t0 + n)], in_=y[:])
+
+        def adds(q, at_once):
+            j = 0
+            pieces[q] = []
+            for n in cut(q):
+                g, t0 = where[QT * q + j]
+                y = ypool.tile([P, n * D], F32, tag="y", name="y")
+                for i in range(n):
+                    nc.vector.tensor_tensor(
+                        out=y[:, D * i : D * i + D], in0=accs[(q, j)][:], in1=bias_bc[:], op=ADD
+                    )
+                    j += 1
+                piece = (y, g, t0, n)
+                if at_once:
+                    finish(piece)
+                else:
+                    pieces[q].append(piece)
+
+        for s in range(1 - LC, NQ):
+            if s < 0:
+                ahead = [s + LC - 1]
+            elif s == 0:
+                ahead = [LC - 1, LC]
+            else:
+                ahead = [s + LC]
+            ahead = [q for q in ahead if q < NQ]
+            if s == 0:
+                bias_ps = psum.tile([P, D], F32, tag="mm", name="bias_ps")
+                nc.tensor.matmul(out=bias_ps[:], lhsT=ones[:], rhs=bz[:], start=True, stop=True)
+                nc.scalar.copy(out=bias_bc[:], in_=bias_ps[:])
+            if s >= 0:
+                passes(s)
+            for q in ahead:
+                transposes(q)
+            if s >= 1:
+                for piece in pieces[s - 1]:
+                    finish(piece)
+            for q in ahead:
+                copies(q, False)
+            if s >= 0:
+                adds(s, s >= NQ - LC)
+            for q in ahead:
+                copies(q, True)
+            if s == -1:
+                quantise(0)
+                quantise(1)
+            elif s >= 0 and s + 2 < NQ:
+                quantise(s + 2)

@@ -11,6 +11,8 @@ U8 = mybir.dt.uint8
 FP8X4 = mybir.dt.float8_e4m3fn_x4
 ADD = mybir.AluOpType.add
 MULT = mybir.AluOpType.mult
+IS_GE = mybir.AluOpType.is_ge
+IS_LE = mybir.AluOpType.is_le
 TANH = mybir.ActivationFunctionType.Tanh
 
 P = 128
@@ -18,14 +20,16 @@ B = 8192
 D = 512
 FLOPS = 2 * B * D * D
 
-MANUAL = True
-GROUP_TILES = [2, 2, 4] + [8] * 7
+GROUP_TILES = [2, 2, 2, 2, 4, 4] + [8] * 6
 NT = B // P
 QT = 4
 NQ = NT // QT
 LC = 4
-V_COPY = ((6, 1), (9, 1), (12, 1), (15, 1))
-Y_BUFS = 8
+PRE = 3
+V_COPY = ((5, 1), (7, 1), (9, 1), (11, 1), (13, 1))
+Y_BUFS = 16
+WB = 264
+W_COL0 = (0, 248)
 
 
 def tile_compositional_t_kernel(tc, x, W, b, units_per_sublayer, graph_distance, out):
@@ -40,26 +44,19 @@ def tile_compositional_t_kernel(tc, x, W, b, units_per_sublayer, graph_distance,
         qpool = ctx.enter_context(tc.tile_pool(name="qpool", bufs=4))
         ypool = ctx.enter_context(tc.tile_pool(name="ypool", bufs=Y_BUFS))
         psum = ctx.enter_context(tc.psum_pool(name="psum", bufs=4))
-        if MANUAL:
-            ctx.enter_context(tc.manual_schedule())
+        ctx.enter_context(tc.manual_schedule())
 
-        bz = const.tile([P, D], BF16, name="bz")
-        nc.vector.memset(bz[:].bitcast(I32), 0)
-        nc.scalar.dma_start(out=bz[0:1, :], in_=b.rearrange("(o n) -> o n", o=1))
+        b_row = const.tile([1, D], BF16, name="b_row")
+        nc.sync.dma_start(out=b_row[:], in_=b.rearrange("(o n) -> o n", o=1))
 
-        ident = const.tile([P, P], F32, name="ident")
-        make_identity(nc, ident[:])
-
-        warm_in = const.tile([P, 1], F32, name="warm_in")
-        warm_out = const.tile([P, 1], F32, name="warm_out")
-        nc.vector.memset(warm_in[:], 0.0)
-        nc.scalar.activation(out=warm_out[:], in_=warm_in[:], func=TANH)
-
-        wt = const.tile([P, 4 * D], BF16, name="wt")
-        nc.sync.dma_start(
-            out=wt[:].rearrange("p (u f) -> p u f", u=2),
-            in_=W.rearrange("(u q e) c -> q u (e c)", u=2, e=2),
-        )
+        wc = const.tile([P, 4 * WB], BF16, name="wc")
+        for u in range(2):
+            nc.sync.dma_start(
+                out=wc[:, 2 * WB * u : 2 * WB * (u + 1)].rearrange("p (e i) -> p e i", e=2),
+                in_=W[256 * u : 256 * (u + 1), W_COL0[u] : W_COL0[u] + WB].rearrange(
+                    "(q e) c -> q e c", e=2
+                ),
+            )
         xs = []
         out_views = []
         where = []
@@ -73,36 +70,47 @@ def tile_compositional_t_kernel(tc, x, W, b, units_per_sublayer, graph_distance,
             where.extend([(g, t) for t in range(tiles)])
             row0 += P * tiles
 
+        zi = const.tile([P, 288], I32, name="zi")
+        nc.gpsimd.iota(zi[:], pattern=[[1, 288]], base=-16, channel_multiplier=-2)
+        ident = const.tile([P, P], F32, name="ident")
+        make_identity(nc, ident[:])
+
+        warm_in = const.tile([P, 1], F32, name="warm_in")
+        warm_out = const.tile([P, 1], F32, name="warm_out")
+        nc.vector.memset(warm_in[:], 0.0)
+        nc.scalar.activation(out=warm_out[:], in_=warm_in[:], func=TANH)
+
         ones = const.tile([P, P], BF16, name="ones")
         nc.vector.memset(ones[:], 1.0)
-        e1 = const.tile([P, 288], BF16, name="e1")
-        nc.vector.memset(e1[:].bitcast(I32), 0)
-        mask = const.tile([P, 4 * D], BF16, name="mask")
-        nc.vector.memset(mask[:].bitcast(I32), 0)
-        nc.vector.tensor_copy(
-            out=e1[:, 16:272].rearrange("p (c two) -> p c two", two=2)[:, :, 0], in_=ident[:]
-        )
-        b2 = const.tile([P, 288], BF16, name="b2")
-        b4 = const.tile([P, 288], BF16, name="b4")
-        b8 = const.tile([P, 288], BF16, name="b8")
-        b9 = const.tile([P, 288], BF16, name="b9")
-        nc.vector.tensor_tensor(out=b2[:, 0:278], in0=e1[:, 0:278], in1=e1[:, 1:279], op=ADD)
-        nc.vector.tensor_tensor(out=b4[:, 0:276], in0=b2[:, 0:276], in1=b2[:, 2:278], op=ADD)
-        nc.vector.tensor_tensor(out=b8[:, 0:272], in0=b4[:, 0:272], in1=b4[:, 4:276], op=ADD)
-        nc.vector.tensor_tensor(out=b9[:, 0:272], in0=b8[:, 0:272], in1=e1[:, 8:280], op=ADD)
-        nc.vector.tensor_copy(out=mask[:, 0:256], in_=b9[:, 16:272])
-        nc.vector.tensor_copy(out=mask[:, 512:768], in_=b9[:, 15:271])
-        nc.vector.tensor_copy(out=mask[:, 1272:1536], in_=b9[:, 8:272])
-        nc.vector.tensor_copy(out=mask[:, 1784:2048], in_=b9[:, 7:271])
+        bz = const.tile([P, D], BF16, name="bz")
+        nc.vector.memset(bz[:].bitcast(I32), 0)
 
-        bias_bc = const.tile([P, D], F32, name="bias_bc")
-
-        nc.vector.tensor_tensor(out=wt[:], in0=wt[:], in1=mask[:], op=MULT)
         wg = const.tile([P, 4 * D], BF16, name="wg", align_bytes=64)
-        nc.vector.tensor_copy(
-            out=wg[:].rearrange("p (c i t) -> p c t i", i=4, t=4),
-            in_=wt[:].rearrange("p (t c i) -> p c t i", t=4, i=4),
+        nc.vector.memset(wg[:].bitcast(I32), 0)
+        ge = const.tile([P, 288], BF16, name="ge")
+        nc.vector.tensor_scalar(out=ge[:], in0=zi[:], scalar1=-8.0, scalar2=None, op0=IS_GE)
+        band = const.tile([P, 2, 288], BF16, name="band")
+        nc.vector.scalar_tensor_tensor(
+            out=band[:, 0, :], in0=zi[:], scalar=0.0, in1=ge[:], op0=IS_LE, op1=MULT
         )
+        nc.vector.tensor_copy(out=band[:, 1, 1:288], in_=band[:, 0, 0:287])
+
+        nc.vector.tensor_copy(out=bz[0:1, :], in_=b_row[:])
+        bias_ps = psum.tile([P, D], F32, tag="mm", name="bias_ps")
+        nc.tensor.matmul(out=bias_ps[:], lhsT=ones[:], rhs=bz[:], start=True, stop=True)
+        bias_bc = const.tile([P, D], F32, name="bias_bc")
+        nc.scalar.copy(out=bias_bc[:], in_=bias_ps[:])
+
+        wg3 = wg[:].rearrange("p (c t) -> p c t", t=4)
+        for u in range(2):
+            half = wc[:, 2 * WB * u : 2 * WB * (u + 1)].rearrange("p (e i) -> p e i", e=2)
+            first = 16 - 8 * u
+            nc.vector.tensor_tensor(out=half, in0=half, in1=band[:, :, first : first + WB], op=MULT)
+        for u in range(2):
+            nc.vector.tensor_copy(
+                out=wg3[:, W_COL0[u] : W_COL0[u] + WB, 2 * u : 2 * u + 2],
+                in_=wc[:, 2 * WB * u : 2 * WB * (u + 1)].rearrange("p (e i) -> p i e", e=2),
+            )
         w_codes = const.tile([P, D], U32, name="w_codes", align_bytes=64)
         w_scales = const.tile([P, D], U8, name="w_scales", align_bytes=64)
         nc.vector.quantize_mx(out=w_codes[:].bitcast(FP8X4), scales=w_scales[:], in_=wg[:])
@@ -158,51 +166,49 @@ def tile_compositional_t_kernel(tc, x, W, b, units_per_sublayer, graph_distance,
                     stop=True,
                 )
 
-        def cut(q):
-            if q == NQ - 1:
-                sizes = [2, 1, 1]
-            elif q >= NQ - LC:
-                sizes = [2, 2]
-            elif where[QT * q][0] != where[QT * q + QT - 1][0]:
-                sizes = [2, 2]
-            else:
-                sizes = [4]
-            return sizes
-
         def finish(piece):
-            y, g, t0, n = piece
+            y, g, first, width = piece
             nc.scalar.activation(out=y[:], in_=y[:], func=TANH)
-            nc.sync.dma_start(out=out_views[g][:, D * t0 : D * (t0 + n)], in_=y[:])
+            nc.sync.dma_start(out=out_views[g][:, first : first + width], in_=y[:])
+
+        def widths(q):
+            if q == NQ - 1:
+                return [512, 512, 512, 256, 256]
+            if q == NQ - 2:
+                return [512, 512, 512, 512]
+            return [1024, 1024]
 
         def adds(q, at_once):
-            j = 0
+            pos = 0
             pieces[q] = []
-            for n in cut(q):
-                g, t0 = where[QT * q + j]
-                y = ypool.tile([P, n * D], F32, tag="y", name="y")
-                for i in range(n):
+            for width in widths(q):
+                g, t0 = where[QT * q + pos // D]
+                y = ypool.tile([P, width], F32, tag="y", name="y")
+                step = min(width, D)
+                for off in range(0, width, step):
+                    j = (pos + off) // D
+                    c0 = (pos + off) % D
                     nc.vector.tensor_tensor(
-                        out=y[:, D * i : D * i + D], in0=accs[(q, j)][:], in1=bias_bc[:], op=ADD
+                        out=y[:, off : off + step],
+                        in0=accs[(q, j)][:, c0 : c0 + step],
+                        in1=bias_bc[:, c0 : c0 + step],
+                        op=ADD,
                     )
-                    j += 1
-                piece = (y, g, t0, n)
+                piece = (y, g, D * t0 + pos % D, width)
+                pos += width
                 if at_once:
                     finish(piece)
                 else:
                     pieces[q].append(piece)
 
-        for s in range(1 - LC, NQ):
+        for s in range(-PRE, NQ):
             if s < 0:
-                ahead = [s + LC - 1]
+                ahead = [s + PRE]
             elif s == 0:
-                ahead = [LC - 1, LC]
+                ahead = list(range(PRE, LC + 1))
             else:
                 ahead = [s + LC]
             ahead = [q for q in ahead if q < NQ]
-            if s == 0:
-                bias_ps = psum.tile([P, D], F32, tag="mm", name="bias_ps")
-                nc.tensor.matmul(out=bias_ps[:], lhsT=ones[:], rhs=bz[:], start=True, stop=True)
-                nc.scalar.copy(out=bias_bc[:], in_=bias_ps[:])
             if s >= 0:
                 passes(s)
             for q in ahead:

@@ -20,14 +20,15 @@ B = 8192
 D = 512
 FLOPS = 2 * B * D * D
 
-GROUP_TILES = [2, 2, 2, 2, 4, 4] + [8] * 6
+GT = 8
+LOAD_TILES = [2, 2, 2, 2, 4, 4] + [8] * 6
+STORE_TILES = [8, 8, 8, 8, 4, 4, 4] + [2] * 9 + [1, 0.5, 0.5]
 NT = B // P
 QT = 4
 NQ = NT // QT
 LC = 4
 PRE = 3
 V_COPY = ((5, 1), (7, 1), (9, 1), (11, 1), (13, 1))
-Y_BUFS = 16
 WB = 264
 W_COL0 = (0, 248)
 
@@ -35,14 +36,14 @@ W_COL0 = (0, 248)
 def tile_compositional_t_kernel(tc, x, W, b, units_per_sublayer, graph_distance, out):
     nc = tc.nc
     assert units_per_sublayer == 1 and graph_distance == 8
-    assert sum(GROUP_TILES) == NT
+    assert sum(LOAD_TILES) == NT and sum(STORE_TILES) == NT
 
     with ExitStack() as ctx:
         const = ctx.enter_context(tc.tile_pool(name="const", bufs=1))
         xpool = ctx.enter_context(tc.tile_pool(name="xpool", bufs=1))
         gpool = ctx.enter_context(tc.tile_pool(name="gpool", bufs=4))
         qpool = ctx.enter_context(tc.tile_pool(name="qpool", bufs=4))
-        ypool = ctx.enter_context(tc.tile_pool(name="ypool", bufs=Y_BUFS))
+        ypool = ctx.enter_context(tc.tile_pool(name="ypool", bufs=1))
         psum = ctx.enter_context(tc.psum_pool(name="psum", bufs=4))
         ctx.enter_context(tc.manual_schedule())
 
@@ -57,18 +58,23 @@ def tile_compositional_t_kernel(tc, x, W, b, units_per_sublayer, graph_distance,
                     "(q e) c -> q e c", e=2
                 ),
             )
+        x_views = x.rearrange("(g p t) k -> g p (t k)", p=P, t=GT)
+        out_views = out.rearrange("(g p t) n -> g p (t n)", p=P, t=GT)
         xs = []
-        out_views = []
         where = []
-        row0 = 0
-        for g, tiles in enumerate(GROUP_TILES):
-            rows = slice(row0, row0 + P * tiles)
-            xg = xpool.tile([P, tiles * D], BF16, name="x%d" % g)
-            nc.sync.dma_start(out=xg[:], in_=x[rows, :].rearrange("(p t) k -> p (t k)", t=tiles))
+        m0 = 0
+        for i, tiles in enumerate(LOAD_TILES):
+            xg = xpool.tile([P, tiles * D], BF16, name="x%d" % i)
+            c0 = (m0 % GT) * D
+            nc.sync.dma_start(out=xg[:], in_=x_views[m0 // GT, :, c0 : c0 + tiles * D])
             xs.append(xg)
-            out_views.append(out[rows, :].rearrange("(p t) n -> p (t n)", t=tiles))
-            where.extend([(g, t) for t in range(tiles)])
-            row0 += P * tiles
+            where.extend([(i, t) for t in range(tiles)])
+            m0 += tiles
+        stores = []
+        col = 0
+        for tiles in STORE_TILES:
+            stores.append([col, int(tiles * D), None])
+            col += int(tiles * D)
 
         zi = const.tile([P, 288], I32, name="zi")
         nc.gpsimd.iota(zi[:], pattern=[[1, 288]], base=-16, channel_multiplier=-2)
@@ -167,9 +173,16 @@ def tile_compositional_t_kernel(tc, x, W, b, units_per_sublayer, graph_distance,
                 )
 
         def finish(piece):
-            y, g, first, width = piece
-            nc.scalar.activation(out=y[:], in_=y[:], func=TANH)
-            nc.sync.dma_start(out=out_views[g][:, first : first + width], in_=y[:])
+            st, first, width = piece
+            s0, s_width, y = st
+            nc.scalar.activation(
+                out=y[:, first - s0 : first - s0 + width],
+                in_=y[:, first - s0 : first - s0 + width],
+                func=TANH,
+            )
+            if first + width == s0 + s_width:
+                c0 = s0 % (GT * D)
+                nc.sync.dma_start(out=out_views[s0 // (GT * D), :, c0 : c0 + s_width], in_=y[:])
 
         def widths(q):
             if q == NQ - 1:
@@ -182,19 +195,27 @@ def tile_compositional_t_kernel(tc, x, W, b, units_per_sublayer, graph_distance,
             pos = 0
             pieces[q] = []
             for width in widths(q):
-                g, t0 = where[QT * q + pos // D]
-                y = ypool.tile([P, width], F32, tag="y", name="y")
+                first = QT * D * q + pos
+                st = [e for e in stores if e[0] <= first < e[0] + e[1]][0]
+                if st[2] is None:
+                    if st[1] > QT * D:
+                        st[2] = ypool.tile([P, st[1]], F32, tag="y_big", name="y_big", bufs=3)
+                    elif st[1] == QT * D:
+                        st[2] = ypool.tile([P, st[1]], F32, tag="y_mid", name="y_mid", bufs=4)
+                    else:
+                        st[2] = ypool.tile([P, st[1]], F32, tag="y_small", name="y_small", bufs=8)
+                y = st[2]
                 step = min(width, D)
                 for off in range(0, width, step):
                     j = (pos + off) // D
                     c0 = (pos + off) % D
                     nc.vector.tensor_tensor(
-                        out=y[:, off : off + step],
+                        out=y[:, first - st[0] + off : first - st[0] + off + step],
                         in0=accs[(q, j)][:, c0 : c0 + step],
                         in1=bias_bc[:, c0 : c0 + step],
                         op=ADD,
                     )
-                piece = (y, g, D * t0 + pos % D, width)
+                piece = (st, first, width)
                 pos += width
                 if at_once:
                     finish(piece)

@@ -20,15 +20,15 @@ B = 8192
 D = 512
 FLOPS = 2 * B * D * D
 
-GT = 8
-LOAD_TILES = [2, 2, 2, 2, 4, 4] + [8] * 6
-STORE_TILES = [8, 8, 8, 8, 4, 4, 4] + [2] * 9 + [1, 0.5, 0.5]
+GROUP_TILES = [2, 2, 2, 2, 4, 4] + [8] * 6
 NT = B // P
 QT = 4
 NQ = NT // QT
 LC = 4
 PRE = 3
 V_COPY = ((5, 1), (7, 1), (9, 1), (11, 1), (13, 1))
+Y_BUFS = 16
+N_WARM = 5
 WB = 264
 W_COL0 = (0, 248)
 
@@ -36,14 +36,14 @@ W_COL0 = (0, 248)
 def tile_compositional_t_kernel(tc, x, W, b, units_per_sublayer, graph_distance, out):
     nc = tc.nc
     assert units_per_sublayer == 1 and graph_distance == 8
-    assert sum(LOAD_TILES) == NT and sum(STORE_TILES) == NT
+    assert sum(GROUP_TILES) == NT
 
     with ExitStack() as ctx:
         const = ctx.enter_context(tc.tile_pool(name="const", bufs=1))
         xpool = ctx.enter_context(tc.tile_pool(name="xpool", bufs=1))
         gpool = ctx.enter_context(tc.tile_pool(name="gpool", bufs=4))
         qpool = ctx.enter_context(tc.tile_pool(name="qpool", bufs=4))
-        ypool = ctx.enter_context(tc.tile_pool(name="ypool", bufs=1))
+        ypool = ctx.enter_context(tc.tile_pool(name="ypool", bufs=Y_BUFS))
         psum = ctx.enter_context(tc.psum_pool(name="psum", bufs=4))
         ctx.enter_context(tc.manual_schedule())
 
@@ -58,23 +58,18 @@ def tile_compositional_t_kernel(tc, x, W, b, units_per_sublayer, graph_distance,
                     "(q e) c -> q e c", e=2
                 ),
             )
-        x_views = x.rearrange("(g p t) k -> g p (t k)", p=P, t=GT)
-        out_views = out.rearrange("(g p t) n -> g p (t n)", p=P, t=GT)
         xs = []
+        out_views = []
         where = []
-        m0 = 0
-        for i, tiles in enumerate(LOAD_TILES):
-            xg = xpool.tile([P, tiles * D], BF16, name="x%d" % i)
-            c0 = (m0 % GT) * D
-            nc.sync.dma_start(out=xg[:], in_=x_views[m0 // GT, :, c0 : c0 + tiles * D])
+        row0 = 0
+        for g, tiles in enumerate(GROUP_TILES):
+            rows = slice(row0, row0 + P * tiles)
+            xg = xpool.tile([P, tiles * D], BF16, name="x%d" % g)
+            nc.sync.dma_start(out=xg[:], in_=x[rows, :].rearrange("(p t) k -> p (t k)", t=tiles))
             xs.append(xg)
-            where.extend([(i, t) for t in range(tiles)])
-            m0 += tiles
-        stores = []
-        col = 0
-        for tiles in STORE_TILES:
-            stores.append([col, int(tiles * D), None])
-            col += int(tiles * D)
+            out_views.append(out[rows, :].rearrange("(p t) n -> p (t n)", t=tiles))
+            where.extend([(g, t) for t in range(tiles)])
+            row0 += P * tiles
 
         zi = const.tile([P, 288], I32, name="zi")
         nc.gpsimd.iota(zi[:], pattern=[[1, 288]], base=-16, channel_multiplier=-2)
@@ -91,6 +86,13 @@ def tile_compositional_t_kernel(tc, x, W, b, units_per_sublayer, graph_distance,
         bz = const.tile([P, D], BF16, name="bz")
         nc.vector.memset(bz[:].bitcast(I32), 0)
 
+        if N_WARM:
+            zeros = const.tile([P, D], BF16, name="zeros")
+            nc.vector.memset(zeros[:].bitcast(I32), 0)
+            warm_ps = psum.tile([P, D], F32, tag="mm", name="warm_ps")
+            for i in range(N_WARM):
+                nc.tensor.matmul(out=warm_ps[:], lhsT=ones[:], rhs=zeros[:], start=True, stop=True)
+
         wg = const.tile([P, 4 * D], BF16, name="wg", align_bytes=64)
         nc.vector.memset(wg[:].bitcast(I32), 0)
         ge = const.tile([P, 288], BF16, name="ge")
@@ -101,11 +103,7 @@ def tile_compositional_t_kernel(tc, x, W, b, units_per_sublayer, graph_distance,
         )
         nc.vector.tensor_copy(out=band[:, 1, 1:288], in_=band[:, 0, 0:287])
 
-        nc.vector.tensor_copy(out=bz[0:1, :], in_=b_row[:])
-        bias_ps = psum.tile([P, D], F32, tag="mm", name="bias_ps")
-        nc.tensor.matmul(out=bias_ps[:], lhsT=ones[:], rhs=bz[:], start=True, stop=True)
         bias_bc = const.tile([P, D], F32, name="bias_bc")
-        nc.scalar.copy(out=bias_bc[:], in_=bias_ps[:])
 
         wg3 = wg[:].rearrange("p (c t) -> p c t", t=4)
         for u in range(2):
@@ -120,6 +118,7 @@ def tile_compositional_t_kernel(tc, x, W, b, units_per_sublayer, graph_distance,
         w_codes = const.tile([P, D], U32, name="w_codes", align_bytes=64)
         w_scales = const.tile([P, D], U8, name="w_scales", align_bytes=64)
         nc.vector.quantize_mx(out=w_codes[:].bitcast(FP8X4), scales=w_scales[:], in_=wg[:])
+        nc.vector.tensor_copy(out=bz[0:1, :], in_=b_row[:])
 
         banks = {}
         grouped = {}
@@ -173,16 +172,9 @@ def tile_compositional_t_kernel(tc, x, W, b, units_per_sublayer, graph_distance,
                 )
 
         def finish(piece):
-            st, first, width = piece
-            s0, s_width, y = st
-            nc.scalar.activation(
-                out=y[:, first - s0 : first - s0 + width],
-                in_=y[:, first - s0 : first - s0 + width],
-                func=TANH,
-            )
-            if first + width == s0 + s_width:
-                c0 = s0 % (GT * D)
-                nc.sync.dma_start(out=out_views[s0 // (GT * D), :, c0 : c0 + s_width], in_=y[:])
+            y, g, first, width = piece
+            nc.scalar.activation(out=y[:], in_=y[:], func=TANH)
+            nc.sync.dma_start(out=out_views[g][:, first : first + width], in_=y[:])
 
         def widths(q):
             if q == NQ - 1:
@@ -195,27 +187,19 @@ def tile_compositional_t_kernel(tc, x, W, b, units_per_sublayer, graph_distance,
             pos = 0
             pieces[q] = []
             for width in widths(q):
-                first = QT * D * q + pos
-                st = [e for e in stores if e[0] <= first < e[0] + e[1]][0]
-                if st[2] is None:
-                    if st[1] > QT * D:
-                        st[2] = ypool.tile([P, st[1]], F32, tag="y_big", name="y_big", bufs=3)
-                    elif st[1] == QT * D:
-                        st[2] = ypool.tile([P, st[1]], F32, tag="y_mid", name="y_mid", bufs=4)
-                    else:
-                        st[2] = ypool.tile([P, st[1]], F32, tag="y_small", name="y_small", bufs=8)
-                y = st[2]
+                g, t0 = where[QT * q + pos // D]
+                y = ypool.tile([P, width], F32, tag="y", name="y")
                 step = min(width, D)
                 for off in range(0, width, step):
                     j = (pos + off) // D
                     c0 = (pos + off) % D
                     nc.vector.tensor_tensor(
-                        out=y[:, first - st[0] + off : first - st[0] + off + step],
+                        out=y[:, off : off + step],
                         in0=accs[(q, j)][:, c0 : c0 + step],
                         in1=bias_bc[:, c0 : c0 + step],
                         op=ADD,
                     )
-                piece = (st, first, width)
+                piece = (y, g, D * t0 + pos % D, width)
                 pos += width
                 if at_once:
                     finish(piece)
@@ -230,10 +214,16 @@ def tile_compositional_t_kernel(tc, x, W, b, units_per_sublayer, graph_distance,
             else:
                 ahead = [s + LC]
             ahead = [q for q in ahead if q < NQ]
+            if s == -1:
+                bias_ps = psum.tile([P, D], F32, tag="mm", name="bias_ps")
+                nc.tensor.matmul(out=bias_ps[:], lhsT=ones[:], rhs=bz[:], start=True, stop=True)
+                nc.scalar.copy(out=bias_bc[:], in_=bias_ps[:])
             if s >= 0:
                 passes(s)
             for q in ahead:
                 transposes(q)
+            if N_WARM and s == -PRE:
+                nc.tensor.matmul(out=warm_ps[:], lhsT=ones[:], rhs=zeros[:], start=True, stop=True)
             if s >= 1:
                 for piece in pieces[s - 1]:
                     finish(piece)

@@ -27,7 +27,7 @@ NQ = NT // QT
 LC = 4
 PRE = 3
 V_COPY = ((5, 1), (7, 1), (9, 1), (11, 1), (13, 1))
-Y_BUFS = 16
+Y_BUFS = {2048: 8, 1024: 8, 512: 9, 256: 2}
 N_WARM = 5
 WB = 264
 W_COL0 = (0, 248)
@@ -43,7 +43,7 @@ def tile_compositional_t_kernel(tc, x, W, b, units_per_sublayer, graph_distance,
         xpool = ctx.enter_context(tc.tile_pool(name="xpool", bufs=1))
         gpool = ctx.enter_context(tc.tile_pool(name="gpool", bufs=4))
         qpool = ctx.enter_context(tc.tile_pool(name="qpool", bufs=4))
-        ypool = ctx.enter_context(tc.tile_pool(name="ypool", bufs=Y_BUFS))
+        ypool = ctx.enter_context(tc.tile_pool(name="ypool", bufs=1))
         psum = ctx.enter_context(tc.psum_pool(name="psum", bufs=4))
         ctx.enter_context(tc.manual_schedule())
 
@@ -181,14 +181,16 @@ def tile_compositional_t_kernel(tc, x, W, b, units_per_sublayer, graph_distance,
                 return [512, 512, 512, 256, 256]
             if q == NQ - 2:
                 return [512, 512, 512, 512]
-            return [1024, 1024]
+            if q < 2 or q >= NQ - 4:
+                return [1024, 1024]
+            return [2048]
 
         def adds(q, at_once):
             pos = 0
             pieces[q] = []
             for width in widths(q):
                 g, t0 = where[QT * q + pos // D]
-                y = ypool.tile([P, width], F32, tag="y", name="y")
+                y = ypool.tile([P, width], F32, tag="y%d" % width, name="y", bufs=Y_BUFS[width])
                 step = min(width, D)
                 for off in range(0, width, step):
                     j = (pos + off) // D

@@ -181,7 +181,7 @@ def tile_compositional_t_kernel(tc, x, W, b, units_per_sublayer, graph_distance,
                 return [512, 512, 512, 256, 256]
             if q == NQ - 2:
                 return [512, 512, 512, 512]
-            if q < 2 or q >= NQ - 4:
+            if q < 2 or q >= NQ - 7:
                 return [1024, 1024]
             return [2048]
 

@@ -12,7 +12,6 @@ FP8X4 = mybir.dt.float8_e4m3fn_x4
 ADD = mybir.AluOpType.add
 MULT = mybir.AluOpType.mult
 IS_GE = mybir.AluOpType.is_ge
-IS_LE = mybir.AluOpType.is_le
 TANH = mybir.ActivationFunctionType.Tanh
 
 P = 128
@@ -20,15 +19,14 @@ B = 8192
 D = 512
 FLOPS = 2 * B * D * D
 
-GROUP_TILES = [2, 2, 2, 2, 4, 4] + [8] * 6
+GROUP_TILES = [2] * 8 + [4, 4, 8, 8, 8, 16]
 NT = B // P
 QT = 4
 NQ = NT // QT
 LC = 4
-PRE = 3
-V_COPY = ((5, 1), (7, 1), (9, 1), (11, 1), (13, 1))
-Y_BUFS = {2048: 8, 1024: 8, 512: 9, 256: 2}
-N_WARM = 5
+V_COPY = tuple((q, 1) for q in range(5, 14, 2))
+Y_BUFS = {2048: 5, 1024: 18, 512: 7, 256: 2}
+N_WARM = 4
 WB = 264
 W_COL0 = (0, 248)
 
@@ -49,7 +47,6 @@ def tile_compositional_t_kernel(tc, x, W, b, units_per_sublayer, graph_distance,
 
         b_row = const.tile([1, D], BF16, name="b_row")
         nc.sync.dma_start(out=b_row[:], in_=b.rearrange("(o n) -> o n", o=1))
-
         wc = const.tile([P, 4 * WB], BF16, name="wc")
         for u in range(2):
             nc.sync.dma_start(
@@ -71,8 +68,6 @@ def tile_compositional_t_kernel(tc, x, W, b, units_per_sublayer, graph_distance,
             where.extend([(g, t) for t in range(tiles)])
             row0 += P * tiles
 
-        zi = const.tile([P, 288], I32, name="zi")
-        nc.gpsimd.iota(zi[:], pattern=[[1, 288]], base=-16, channel_multiplier=-2)
         ident = const.tile([P, P], F32, name="ident")
         make_identity(nc, ident[:])
 
@@ -83,9 +78,6 @@ def tile_compositional_t_kernel(tc, x, W, b, units_per_sublayer, graph_distance,
 
         ones = const.tile([P, P], BF16, name="ones")
         nc.vector.memset(ones[:], 1.0)
-        bz = const.tile([P, D], BF16, name="bz")
-        nc.vector.memset(bz[:].bitcast(I32), 0)
-
         if N_WARM:
             zeros = const.tile([P, D], BF16, name="zeros")
             nc.vector.memset(zeros[:].bitcast(I32), 0)
@@ -93,17 +85,31 @@ def tile_compositional_t_kernel(tc, x, W, b, units_per_sublayer, graph_distance,
             for i in range(N_WARM):
                 nc.tensor.matmul(out=warm_ps[:], lhsT=ones[:], rhs=zeros[:], start=True, stop=True)
 
-        wg = const.tile([P, 4 * D], BF16, name="wg", align_bytes=64)
-        nc.vector.memset(wg[:].bitcast(I32), 0)
-        ge = const.tile([P, 288], BF16, name="ge")
-        nc.vector.tensor_scalar(out=ge[:], in0=zi[:], scalar1=-8.0, scalar2=None, op0=IS_GE)
         band = const.tile([P, 2, 288], BF16, name="band")
-        nc.vector.scalar_tensor_tensor(
-            out=band[:, 0, :], in0=zi[:], scalar=0.0, in1=ge[:], op0=IS_LE, op1=MULT
+        nc.vector.memset(band[:, 0, :], 1.0)
+        nc.gpsimd.affine_select(
+            out=band[:, 0, :], in_=band[:, 0, :], compare_op=IS_GE, fill=0.0,
+            base=16, pattern=[[-1, 288]], channel_multiplier=2,
         )
+        nc.gpsimd.affine_select(
+            out=band[:, 0, :], in_=band[:, 0, :], compare_op=IS_GE, fill=0.0,
+            base=-8, pattern=[[1, 288]], channel_multiplier=-2,
+        )
+
+        bz = const.tile([P, D], BF16, name="bz")
+        nc.vector.memset(bz[:].bitcast(I32), 0)
+
+        wg = const.tile([P, 4 * D], BF16, name="wg", align_bytes=64)
+        wg_pairs = wg[:].bitcast(I32).rearrange("p (c u) -> p c u", u=2)
+        nc.vector.memset(wg_pairs[:, 0 : W_COL0[1], 1], 0)
+        nc.vector.memset(wg_pairs[:, W_COL0[0] + WB : D, 0], 0)
         nc.vector.tensor_copy(out=band[:, 1, 1:288], in_=band[:, 0, 0:287])
 
         bias_bc = const.tile([P, D], F32, name="bias_bc")
+
+        nc.vector.tensor_copy(out=bz[0:1, :], in_=b_row[:])
+        bias_ps = psum.tile([P, D], F32, tag="mm", name="bias_ps")
+        nc.tensor.matmul(out=bias_ps[:], lhsT=ones[:], rhs=bz[:], start=True, stop=True)
 
         wg3 = wg[:].rearrange("p (c t) -> p c t", t=4)
         for u in range(2):
@@ -118,7 +124,6 @@ def tile_compositional_t_kernel(tc, x, W, b, units_per_sublayer, graph_distance,
         w_codes = const.tile([P, D], U32, name="w_codes", align_bytes=64)
         w_scales = const.tile([P, D], U8, name="w_scales", align_bytes=64)
         nc.vector.quantize_mx(out=w_codes[:].bitcast(FP8X4), scales=w_scales[:], in_=wg[:])
-        nc.vector.tensor_copy(out=bz[0:1, :], in_=b_row[:])
 
         banks = {}
         grouped = {}
@@ -126,8 +131,8 @@ def tile_compositional_t_kernel(tc, x, W, b, units_per_sublayer, graph_distance,
         accs = {}
         pieces = {}
 
-        def transposes(q):
-            for h in range(2):
+        def transposes(q, halves):
+            for h in halves:
                 tp = psum.tile([P, 2, 2, P], F32, tag="tp", name="tp")
                 banks[(q, h)] = tp
                 for j in range(2):
@@ -149,15 +154,22 @@ def tile_compositional_t_kernel(tc, x, W, b, units_per_sublayer, graph_distance,
                 if not on_vector and (q, h) not in V_COPY:
                     nc.scalar.copy(out=dst, in_=src)
 
-        def quantise(q):
-            cq = qpool.tile([P, QT * P], U32, tag="codes", name="codes", align_bytes=64)
-            sq = qpool.tile([P, QT * P], U8, tag="scales", name="scales", align_bytes=64)
-            codes[q] = (cq, sq)
-            nc.vector.quantize_mx(out=cq[:].bitcast(FP8X4), scales=sq[:], in_=grouped[q][:])
-
-        def passes(q):
+        def quantise(q, first=0, tiles=QT):
+            if first == 0:
+                cq = qpool.tile([P, QT * P], U32, tag="codes", name="codes", align_bytes=64)
+                sq = qpool.tile([P, QT * P], U8, tag="scales", name="scales", align_bytes=64)
+                codes[q] = (cq, sq)
             cq, sq = codes[q]
-            for j in range(QT):
+            cols = slice(P * first, P * (first + tiles))
+            nc.vector.quantize_mx(
+                out=cq[:, cols].bitcast(FP8X4),
+                scales=sq[:, cols],
+                in_=grouped[q][:, D * first : D * (first + tiles)],
+            )
+
+        def passes(q, tiles):
+            cq, sq = codes[q]
+            for j in tiles:
                 acc = psum.tile([P, D], F32, tag="mm", name="acc")
                 accs[(q, j)] = acc
                 cols = slice(P * j, P * j + P)
@@ -181,14 +193,17 @@ def tile_compositional_t_kernel(tc, x, W, b, units_per_sublayer, graph_distance,
                 return [512, 512, 512, 256, 256]
             if q == NQ - 2:
                 return [512, 512, 512, 512]
-            if q < 2 or q >= NQ - 7:
+            if q < 4 or q >= NQ - 7:
                 return [1024, 1024]
             return [2048]
 
-        def adds(q, at_once):
+        def adds(q, at_once, chosen):
             pos = 0
-            pieces[q] = []
-            for width in widths(q):
+            pieces.setdefault(q, [])
+            for n, width in enumerate(widths(q)):
+                if n not in chosen:
+                    pos += width
+                    continue
                 g, t0 = where[QT * q + pos // D]
                 y = ypool.tile([P, width], F32, tag="y%d" % width, name="y", bufs=Y_BUFS[width])
                 step = min(width, D)
@@ -208,35 +223,41 @@ def tile_compositional_t_kernel(tc, x, W, b, units_per_sublayer, graph_distance,
                 else:
                     pieces[q].append(piece)
 
-        for s in range(-PRE, NQ):
-            if s < 0:
-                ahead = [s + PRE]
-            elif s == 0:
-                ahead = list(range(PRE, LC + 1))
-            else:
-                ahead = [s + LC]
-            ahead = [q for q in ahead if q < NQ]
-            if s == -1:
-                bias_ps = psum.tile([P, D], F32, tag="mm", name="bias_ps")
-                nc.tensor.matmul(out=bias_ps[:], lhsT=ones[:], rhs=bz[:], start=True, stop=True)
-                nc.scalar.copy(out=bias_bc[:], in_=bias_ps[:])
-            if s >= 0:
-                passes(s)
+        transposes(0, (0, 1))
+        if N_WARM:
+            nc.tensor.matmul(out=warm_ps[:], lhsT=ones[:], rhs=zeros[:], start=True, stop=True)
+        copies(0, False)
+        transposes(1, (0, 1))
+        copies(1, False)
+        quantise(0, 0, 2)
+        nc.vector.tensor_copy(out=bias_bc[:], in_=bias_ps[:])
+        quantise(0, 2, 2)
+        transposes(2, (0,))
+        passes(0, (0, 1))
+        transposes(2, (1,))
+        copies(2, False)
+        passes(0, (2, 3))
+        adds(0, False, (0,))
+        quantise(1)
+        finish(pieces[0][0])
+        transposes(3, (0, 1))
+        copies(3, False)
+        adds(0, False, (1,))
+        quantise(2)
+        for s in range(1, NQ):
+            ahead = [q for q in ([4, 5] if s == 1 else [s + LC]) if q < NQ]
+            passes(s, range(QT))
             for q in ahead:
-                transposes(q)
-            if N_WARM and s == -PRE:
-                nc.tensor.matmul(out=warm_ps[:], lhsT=ones[:], rhs=zeros[:], start=True, stop=True)
-            if s >= 1:
+                transposes(q, (0, 1))
+            if s == 1:
+                finish(pieces[0][1])
+            else:
                 for piece in pieces[s - 1]:
                     finish(piece)
             for q in ahead:
                 copies(q, False)
-            if s >= 0:
-                adds(s, s >= NQ - LC)
+            adds(s, s >= NQ - LC, range(5))
             for q in ahead:
                 copies(q, True)
-            if s == -1:
-                quantise(0)
-                quantise(1)
-            elif s >= 0 and s + 2 < NQ:
+            if s + 2 < NQ:
                 quantise(s + 2)

@@ -12,6 +12,7 @@ FP8X4 = mybir.dt.float8_e4m3fn_x4
 ADD = mybir.AluOpType.add
 MULT = mybir.AluOpType.mult
 IS_GE = mybir.AluOpType.is_ge
+IS_LE = mybir.AluOpType.is_le
 TANH = mybir.ActivationFunctionType.Tanh
 
 P = 128
@@ -19,13 +20,13 @@ B = 8192
 D = 512
 FLOPS = 2 * B * D * D
 
-GROUP_TILES = [2] * 8 + [4, 4, 8, 8, 8, 16]
+GROUP_TILES = [2, 2, 2, 2, 4, 4] + [8] * 6
 NT = B // P
 QT = 4
 NQ = NT // QT
 LC = 4
 V_COPY = tuple((q, 1) for q in range(5, 14, 2))
-Y_BUFS = {2048: 5, 1024: 18, 512: 7, 256: 2}
+Y_BUFS = {2048: 7, 1024: 14, 512: 7, 256: 2}
 N_WARM = 4
 WB = 264
 W_COL0 = (0, 248)
@@ -68,6 +69,8 @@ def tile_compositional_t_kernel(tc, x, W, b, units_per_sublayer, graph_distance,
             where.extend([(g, t) for t in range(tiles)])
             row0 += P * tiles
 
+        zi = const.tile([P, 288], I32, name="zi")
+        nc.gpsimd.iota(zi[:], pattern=[[1, 288]], base=-16, channel_multiplier=-2)
         ident = const.tile([P, P], F32, name="ident")
         make_identity(nc, ident[:])
 
@@ -85,17 +88,6 @@ def tile_compositional_t_kernel(tc, x, W, b, units_per_sublayer, graph_distance,
             for i in range(N_WARM):
                 nc.tensor.matmul(out=warm_ps[:], lhsT=ones[:], rhs=zeros[:], start=True, stop=True)
 
-        band = const.tile([P, 2, 288], BF16, name="band")
-        nc.vector.memset(band[:, 0, :], 1.0)
-        nc.gpsimd.affine_select(
-            out=band[:, 0, :], in_=band[:, 0, :], compare_op=IS_GE, fill=0.0,
-            base=16, pattern=[[-1, 288]], channel_multiplier=2,
-        )
-        nc.gpsimd.affine_select(
-            out=band[:, 0, :], in_=band[:, 0, :], compare_op=IS_GE, fill=0.0,
-            base=-8, pattern=[[1, 288]], channel_multiplier=-2,
-        )
-
         bz = const.tile([P, D], BF16, name="bz")
         nc.vector.memset(bz[:].bitcast(I32), 0)
 
@@ -103,12 +95,18 @@ def tile_compositional_t_kernel(tc, x, W, b, units_per_sublayer, graph_distance,
         wg_pairs = wg[:].bitcast(I32).rearrange("p (c u) -> p c u", u=2)
         nc.vector.memset(wg_pairs[:, 0 : W_COL0[1], 1], 0)
         nc.vector.memset(wg_pairs[:, W_COL0[0] + WB : D, 0], 0)
+        ge = const.tile([P, 288], BF16, name="ge")
+        nc.vector.tensor_scalar(out=ge[:], in0=zi[:], scalar1=-8.0, scalar2=None, op0=IS_GE)
+        band = const.tile([P, 2, 288], BF16, name="band")
+        nc.vector.scalar_tensor_tensor(
+            out=band[:, 0, :], in0=zi[:], scalar=0.0, in1=ge[:], op0=IS_LE, op1=MULT
+        )
         nc.vector.tensor_copy(out=band[:, 1, 1:288], in_=band[:, 0, 0:287])
 
-        bias_bc = const.tile([P, D], F32, name="bias_bc")
+        bias_bc = const.tile([P, D], BF16, name="bias_bc")
 
         nc.vector.tensor_copy(out=bz[0:1, :], in_=b_row[:])
-        bias_ps = psum.tile([P, D], F32, tag="mm", name="bias_ps")
+        bias_ps = psum.tile([P, D], BF16, tag="mm", name="bias_ps")
         nc.tensor.matmul(out=bias_ps[:], lhsT=ones[:], rhs=bz[:], start=True, stop=True)
 
         wg3 = wg[:].rearrange("p (c t) -> p c t", t=4)
@@ -193,7 +191,7 @@ def tile_compositional_t_kernel(tc, x, W, b, units_per_sublayer, graph_distance,
                 return [512, 512, 512, 256, 256]
             if q == NQ - 2:
                 return [512, 512, 512, 512]
-            if q < 4 or q >= NQ - 7:
+            if q < 2 or q >= NQ - 7:
                 return [1024, 1024]
             return [2048]
 
@@ -227,14 +225,13 @@ def tile_compositional_t_kernel(tc, x, W, b, units_per_sublayer, graph_distance,
         if N_WARM:
             nc.tensor.matmul(out=warm_ps[:], lhsT=ones[:], rhs=zeros[:], start=True, stop=True)
         copies(0, False)
+        nc.scalar.copy(out=bias_bc[:], in_=bias_ps[:])
         transposes(1, (0, 1))
         copies(1, False)
         quantise(0, 0, 2)
-        nc.vector.tensor_copy(out=bias_bc[:], in_=bias_ps[:])
         quantise(0, 2, 2)
-        transposes(2, (0,))
         passes(0, (0, 1))
-        transposes(2, (1,))
+        transposes(2, (0, 1))
         copies(2, False)
         passes(0, (2, 3))
         adds(0, False, (0,))

@@ -27,7 +27,7 @@ NQ = NT // QT
 LC = 4
 V_COPY = tuple((q, 1) for q in range(5, 14, 2))
 Y_BUFS = {2048: 7, 1024: 14, 512: 7, 256: 2}
-N_WARM = 4
+N_WARM = 7
 WB = 264
 W_COL0 = (0, 248)
 

from contextlib import ExitStack

import concourse.mybir as mybir
from concourse.masks import make_identity

F32 = mybir.dt.float32
BF16 = mybir.dt.bfloat16
I32 = mybir.dt.int32
U32 = mybir.dt.uint32
U8 = mybir.dt.uint8
FP8X4 = mybir.dt.float8_e4m3fn_x4
ADD = mybir.AluOpType.add
MULT = mybir.AluOpType.mult
IS_GE = mybir.AluOpType.is_ge
IS_LE = mybir.AluOpType.is_le
TANH = mybir.ActivationFunctionType.Tanh

P = 128
B = 8192
D = 512
FLOPS = 2 * B * D * D

GROUP_TILES = [2, 2, 2, 2, 4, 4] + [8] * 6
NT = B // P
QT = 4
NQ = NT // QT
LC = 4
V_COPY = tuple((q, 1) for q in range(5, 14, 2))
Y_BUFS = {2048: 7, 1024: 14, 512: 7, 256: 2}
N_WARM = 7
WB = 264
W_COL0 = (0, 248)


def tile_compositional_t_kernel(tc, x, W, b, units_per_sublayer, graph_distance, out):
    nc = tc.nc
    assert units_per_sublayer == 1 and graph_distance == 8
    assert sum(GROUP_TILES) == NT

    with ExitStack() as ctx:
        const = ctx.enter_context(tc.tile_pool(name="const", bufs=1))
        xpool = ctx.enter_context(tc.tile_pool(name="xpool", bufs=1))
        gpool = ctx.enter_context(tc.tile_pool(name="gpool", bufs=4))
        qpool = ctx.enter_context(tc.tile_pool(name="qpool", bufs=4))
        ypool = ctx.enter_context(tc.tile_pool(name="ypool", bufs=1))
        psum = ctx.enter_context(tc.psum_pool(name="psum", bufs=4))
        ctx.enter_context(tc.manual_schedule())

        b_row = const.tile([1, D], BF16, name="b_row")
        nc.sync.dma_start(out=b_row[:], in_=b.rearrange("(o n) -> o n", o=1))
        wc = const.tile([P, 4 * WB], BF16, name="wc")
        for u in range(2):
            nc.sync.dma_start(
                out=wc[:, 2 * WB * u : 2 * WB * (u + 1)].rearrange("p (e i) -> p e i", e=2),
                in_=W[256 * u : 256 * (u + 1), W_COL0[u] : W_COL0[u] + WB].rearrange(
                    "(q e) c -> q e c", e=2
                ),
            )
        xs = []
        out_views = []
        where = []
        row0 = 0
        for g, tiles in enumerate(GROUP_TILES):
            rows = slice(row0, row0 + P * tiles)
            xg = xpool.tile([P, tiles * D], BF16, name="x%d" % g)
            nc.sync.dma_start(out=xg[:], in_=x[rows, :].rearrange("(p t) k -> p (t k)", t=tiles))
            xs.append(xg)
            out_views.append(out[rows, :].rearrange("(p t) n -> p (t n)", t=tiles))
            where.extend([(g, t) for t in range(tiles)])
            row0 += P * tiles

        zi = const.tile([P, 288], I32, name="zi")
        nc.gpsimd.iota(zi[:], pattern=[[1, 288]], base=-16, channel_multiplier=-2)
        ident = const.tile([P, P], F32, name="ident")
        make_identity(nc, ident[:])

        warm_in = const.tile([P, 1], F32, name="warm_in")
        warm_out = const.tile([P, 1], F32, name="warm_out")
        nc.vector.memset(warm_in[:], 0.0)
        nc.scalar.activation(out=warm_out[:], in_=warm_in[:], func=TANH)

        ones = const.tile([P, P], BF16, name="ones")
        nc.vector.memset(ones[:], 1.0)
        if N_WARM:
            zeros = const.tile([P, D], BF16, name="zeros")
            nc.vector.memset(zeros[:].bitcast(I32), 0)
            warm_ps = psum.tile([P, D], F32, tag="mm", name="warm_ps")
            for i in range(N_WARM):
                nc.tensor.matmul(out=warm_ps[:], lhsT=ones[:], rhs=zeros[:], start=True, stop=True)

        bz = const.tile([P, D], BF16, name="bz")
        nc.vector.memset(bz[:].bitcast(I32), 0)

        wg = const.tile([P, 4 * D], BF16, name="wg", align_bytes=64)
        wg_pairs = wg[:].bitcast(I32).rearrange("p (c u) -> p c u", u=2)
        nc.vector.memset(wg_pairs[:, 0 : W_COL0[1], 1], 0)
        nc.vector.memset(wg_pairs[:, W_COL0[0] + WB : D, 0], 0)
        ge = const.tile([P, 288], BF16, name="ge")
        nc.vector.tensor_scalar(out=ge[:], in0=zi[:], scalar1=-8.0, scalar2=None, op0=IS_GE)
        band = const.tile([P, 2, 288], BF16, name="band")
        nc.vector.scalar_tensor_tensor(
            out=band[:, 0, :], in0=zi[:], scalar=0.0, in1=ge[:], op0=IS_LE, op1=MULT
        )
        nc.vector.tensor_copy(out=band[:, 1, 1:288], in_=band[:, 0, 0:287])

        bias_bc = const.tile([P, D], BF16, name="bias_bc")

        nc.vector.tensor_copy(out=bz[0:1, :], in_=b_row[:])
        bias_ps = psum.tile([P, D], BF16, tag="mm", name="bias_ps")
        nc.tensor.matmul(out=bias_ps[:], lhsT=ones[:], rhs=bz[:], start=True, stop=True)

        wg3 = wg[:].rearrange("p (c t) -> p c t", t=4)
        for u in range(2):
            half = wc[:, 2 * WB * u : 2 * WB * (u + 1)].rearrange("p (e i) -> p e i", e=2)
            first = 16 - 8 * u
            nc.vector.tensor_tensor(out=half, in0=half, in1=band[:, :, first : first + WB], op=MULT)
        for u in range(2):
            nc.vector.tensor_copy(
                out=wg3[:, W_COL0[u] : W_COL0[u] + WB, 2 * u : 2 * u + 2],
                in_=wc[:, 2 * WB * u : 2 * WB * (u + 1)].rearrange("p (e i) -> p i e", e=2),
            )
        w_codes = const.tile([P, D], U32, name="w_codes", align_bytes=64)
        w_scales = const.tile([P, D], U8, name="w_scales", align_bytes=64)
        nc.vector.quantize_mx(out=w_codes[:].bitcast(FP8X4), scales=w_scales[:], in_=wg[:])

        banks = {}
        grouped = {}
        codes = {}
        accs = {}
        pieces = {}

        def transposes(q, halves):
            for h in halves:
                tp = psum.tile([P, 2, 2, P], F32, tag="tp", name="tp")
                banks[(q, h)] = tp
                for j in range(2):
                    g, t = where[QT * q + 2 * h + j]
                    words = xs[g][:].bitcast(F32)
                    for u in range(2):
                        c0 = 256 * t + P * u
                        nc.tensor.transpose(tp[:, j, u, :], words[:, c0 : c0 + P], ident[:])

        def copies(q, on_vector):
            if q not in grouped:
                grouped[q] = gpool.tile([P, QT * D], BF16, tag="grp", name="grp", align_bytes=64)
            g32 = grouped[q][:].bitcast(F32)
            for h in range(2):
                dst = g32[:, 512 * h : 512 * h + 512].rearrange("p (j r u) -> p j r u", j=2, u=2)
                src = banks[(q, h)][:].rearrange("p j u r -> p j r u")
                if on_vector and (q, h) in V_COPY:
                    nc.vector.tensor_copy(out=dst, in_=src)
                if not on_vector and (q, h) not in V_COPY:
                    nc.scalar.copy(out=dst, in_=src)

        def quantise(q, first=0, tiles=QT):
            if first == 0:
                cq = qpool.tile([P, QT * P], U32, tag="codes", name="codes", align_bytes=64)
                sq = qpool.tile([P, QT * P], U8, tag="scales", name="scales", align_bytes=64)
                codes[q] = (cq, sq)
            cq, sq = codes[q]
            cols = slice(P * first, P * (first + tiles))
            nc.vector.quantize_mx(
                out=cq[:, cols].bitcast(FP8X4),
                scales=sq[:, cols],
                in_=grouped[q][:, D * first : D * (first + tiles)],
            )

        def passes(q, tiles):
            cq, sq = codes[q]
            for j in tiles:
                acc = psum.tile([P, D], F32, tag="mm", name="acc")
                accs[(q, j)] = acc
                cols = slice(P * j, P * j + P)
                nc.tensor.matmul_mx(
                    out=acc[:],
                    lhsT=cq[:, cols].bitcast(FP8X4),
                    lhsT_scale=sq[:, cols],
                    rhs=w_codes[:].bitcast(FP8X4),
                    rhs_scale=w_scales[:],
                    start=True,
                    stop=True,
                )

        def finish(piece):
            y, g, first, width = piece
            nc.scalar.activation(out=y[:], in_=y[:], func=TANH)
            nc.sync.dma_start(out=out_views[g][:, first : first + width], in_=y[:])

        def widths(q):
            if q == NQ - 1:
                return [512, 512, 512, 256, 256]
            if q == NQ - 2:
                return [512, 512, 512, 512]
            if q < 2 or q >= NQ - 7:
                return [1024, 1024]
            return [2048]

        def adds(q, at_once, chosen):
            pos = 0
            pieces.setdefault(q, [])
            for n, width in enumerate(widths(q)):
                if n not in chosen:
                    pos += width
                    continue
                g, t0 = where[QT * q + pos // D]
                y = ypool.tile([P, width], F32, tag="y%d" % width, name="y", bufs=Y_BUFS[width])
                step = min(width, D)
                for off in range(0, width, step):
                    j = (pos + off) // D
                    c0 = (pos + off) % D
                    nc.vector.tensor_tensor(
                        out=y[:, off : off + step],
                        in0=accs[(q, j)][:, c0 : c0 + step],
                        in1=bias_bc[:, c0 : c0 + step],
                        op=ADD,
                    )
                piece = (y, g, D * t0 + pos % D, width)
                pos += width
                if at_once:
                    finish(piece)
                else:
                    pieces[q].append(piece)

        transposes(0, (0, 1))
        if N_WARM:
            nc.tensor.matmul(out=warm_ps[:], lhsT=ones[:], rhs=zeros[:], start=True, stop=True)
        copies(0, False)
        nc.scalar.copy(out=bias_bc[:], in_=bias_ps[:])
        transposes(1, (0, 1))
        copies(1, False)
        quantise(0, 0, 2)
        quantise(0, 2, 2)
        passes(0, (0, 1))
        transposes(2, (0, 1))
        copies(2, False)
        passes(0, (2, 3))
        adds(0, False, (0,))
        quantise(1)
        finish(pieces[0][0])
        transposes(3, (0, 1))
        copies(3, False)
        adds(0, False, (1,))
        quantise(2)
        for s in range(1, NQ):
            ahead = [q for q in ([4, 5] if s == 1 else [s + LC]) if q < NQ]
            passes(s, range(QT))
            for q in ahead:
                transposes(q, (0, 1))
            if s == 1:
                finish(pieces[0][1])
            else:
                for piece in pieces[s - 1]:
                    finish(piece)
            for q in ahead:
                copies(q, False)
            adds(s, s >= NQ - LC, range(5))
            for q in ahead:
                copies(q, True)
            if s + 2 < NQ:
                quantise(s + 2)
